import numpy as np
import ml_dtypes


def mxq(x, axis, fmt="e4m3"):
    dtype, down = {"e4m3": (ml_dtypes.float8_e4m3fn, 7), "e5m2": (ml_dtypes.float8_e5m2, 14)}[fmt]
    v = np.moveaxis(np.asarray(x, np.float32).astype(ml_dtypes.bfloat16).astype(np.float64), axis, -1)
    blocks = v.reshape(v.shape[:-1] + (-1, 32))
    amax = np.abs(blocks).max(-1, keepdims=True)
    byte = np.maximum(np.where(amax > 0, np.frexp(amax)[1] - 1 + 127, 0) - down, 1)
    scale = np.exp2(byte - 127.0)
    codes = (blocks / scale).astype(np.float32).astype(dtype).astype(np.float64)
    return np.moveaxis((codes * scale).reshape(v.shape), -1, axis)


WIDE = False


def mx_kscale(k):
    if not WIDE:
        return np.ones(k)
    levels = np.array([10, -10, 5, -5, 0])
    if k % 512:
        return np.exp2(np.random.permutation(np.resize(levels, k // 32))).repeat(32)
    a = np.empty((k // 512, 16))
    for p in range(k // 512):
        a[p, :8] = np.random.permutation(np.resize(levels, 8))
        for g in range(8):
            far = levels[np.abs(levels - a[p, g]) >= 10]
            a[p, g + 8] = far[np.random.randint(len(far))]
    return np.exp2(a.ravel()).repeat(32)


BF16 = ml_dtypes.bfloat16


def bf(x):
    return np.asarray(x, np.float32).astype(BF16)


def f64(x):
    return np.asarray(x).astype(np.float64)


T, B, I, H = 64, 128, 512, 128


def sigmoid(v):
    return 1.0 / (1.0 + np.exp(-v))


def setup_inputs():
    s = mx_kscale(I)
    return {"input_seq": bf(np.random.standard_normal((T, B, I)) * s),
            "W_ih": bf(np.random.standard_normal((3 * H, I)) / np.sqrt(I) / s[None, :]),
            "b_ih": bf(np.random.standard_normal(3 * H) * 0.3),
            "gh": bf(np.random.standard_normal((B, 3 * H)) * 0.5)}


def reference(input_seq, W_ih, b_ih, gh):
    gi = (mxq(f64(input_seq), 2, "e4m3") @ mxq(f64(W_ih), 1, "e4m3").T) + f64(b_ih)
    g = f64(gh)
    i_r, i_z, i_n = gi[..., :H], gi[..., H:2 * H], gi[..., 2 * H:]
    h_r, h_z, h_n = g[..., :H], g[..., H:2 * H], g[..., 2 * H:]
    r = sigmoid(i_r + h_r)
    z = sigmoid(i_z + h_z)
    n = np.tanh(i_n + r * h_n)
    h = (1.0 - z) * n
    return np.transpose(h, (1, 0, 2))

@@ -1,0 +1,321 @@
+from contextlib import ExitStack
+
+import concourse.mybir as mybir
+from concourse.masks import make_identity
+
+F32 = mybir.dt.float32
+BF16 = mybir.dt.bfloat16
+U32 = mybir.dt.uint32
+U8 = mybir.dt.uint8
+FP8X4 = mybir.dt.float8_e4m3fn_x4
+ACT = mybir.ActivationFunctionType
+ALU = mybir.AluOpType
+
+T, B, I, H = 64, 128, 512, 128
+P = 128
+FLOPS = 2 * T * B * I * 3 * H
+
+NU = 16
+CHUNKS = [2, 2, 4, 8, 8, 8, 8, 8, 8, 8]
+AHEAD = 3
+SCALAR_INPUT_COPIES = ((0, 1), (2, 0))
+SCALAR_RESULT_COPIES = (0, 2, 4, 6, 8, 10)
+
+
+def tile_grucellmodel_pa_t_kernel(tc, input_seq, W_ih, b_ih, gh, out):
+    nc = tc.nc
+    with ExitStack() as ctx:
+        const = ctx.enter_context(tc.tile_pool(name="const", bufs=1))
+        xpool = ctx.enter_context(tc.tile_pool(name="xpool", bufs=1))
+        gpool = ctx.enter_context(tc.tile_pool(name="gpool", bufs=4))
+        work = ctx.enter_context(tc.tile_pool(name="work", bufs=3))
+        psx = ctx.enter_context(tc.psum_pool(name="psx", bufs=2))
+        psg = ctx.enter_context(tc.psum_pool(name="psg", bufs=5))
+        pso = ctx.enter_context(tc.psum_pool(name="pso", bufs=1))
+        ctx.enter_context(tc.manual_schedule())
+
+        zeros = const.tile([P, 512], BF16)
+        nc.vector.memset(zeros[:], 0.0)
+        pwarm = pso.tile([P, 512], F32, tag="po")
+
+        def idle_matmuls(count):
+            for k in range(count):
+                nc.tensor.matmul(out=pwarm[:], lhsT=zeros[:, 0:P], rhs=zeros[:], start=True, stop=True)
+
+        idle_matmuls(8)
+
+        ghb = const.tile([P, 512], BF16)
+        nc.vector.memset(ghb[:, 384:512], 0.0)
+        nc.scalar.dma_start(out=ghb[:, 0:384], in_=gh)
+        nc.scalar.dma_start(out=ghb[0:3, 384:512], in_=b_ih.rearrange("(g h) -> g h", g=3))
+        warm = const.tile([P, 1], F32)
+        nc.vector.memset(warm[:], 0.0)
+        warm2 = const.tile([P, 1], F32)
+        nc.scalar.activation(out=warm2[:], in_=warm[:], func=ACT.Sigmoid)
+        w_sb = const.tile([P, 3 * I], BF16)
+        nc.sync.dma_start(
+            out=w_sb[:].rearrange("p (g k) -> p g k", g=3),
+            in_=W_ih.rearrange("(g p) k -> p g k", g=3),
+        )
+        xflat = input_seq.rearrange("t b k -> (t b k)").rearrange("(p f) -> p f", p=P)
+        half_src = []
+        bb0 = 0
+        for c, nbb in enumerate(CHUNKS):
+            xc = xpool.tile([P, nbb * I], BF16, name="x%d" % c)
+            nc.sync.dma_start(out=xc[:], in_=xflat[:, bb0 * I : (bb0 + nbb) * I])
+            for s in range(nbb // 2):
+                half_src.append((xc[:].bitcast(F32), s * 2 * 256))
+            bb0 += nbb
+        out_view = out.rearrange("b t h -> (b t h)").rearrange(
+            "(q j i f) -> j i q f", q=2, j=NU, i=P
+        )
+
+        ident = const.tile([P, P], F32)
+        make_identity(nc, ident[:])
+        perm = const.tile([P, P], F32)
+        nc.vector.tensor_copy(
+            out=perm[:].rearrange("p (q l h) -> p q l h", q=2, l=2),
+            in_=ident[:].rearrange("p (h l q) -> p q l h", q=2, l=2),
+        )
+
+        ghf = const.tile([P, 512], F32)
+        nc.scalar.copy(out=ghf[:], in_=ghb[:])
+
+        ww = w_sb[:].bitcast(F32)
+        pwa = psg.tile([P, 512], F32, tag="gate")
+        pwb = psg.tile([P, 512], F32, tag="gate")
+        for g in range(3):
+            for u in range(2):
+                dst = pwa[:, (2 * g + u) * P : (2 * g + u + 1) * P] if g < 2 else pwb[:, u * P : (u + 1) * P]
+                nc.tensor.transpose(dst, ww[:, g * 256 + u : (g + 1) * 256 : 2], ident[:])
+        wgrouped = const.tile([P, 3 * I], BF16, align_bytes=64)
+        wgw = wgrouped[:].bitcast(F32)
+        nc.vector.tensor_copy(
+            out=wgw[:, 0:512].rearrange("p (c n u) -> p c n u", c=2, u=2),
+            in_=pwa[:].rearrange("p (c u n) -> p c n u", c=2, u=2),
+        )
+        nc.scalar.copy(
+            out=wgw[:, 512:768].rearrange("p (n u) -> p n u", u=2),
+            in_=pwb[:, 0:256].rearrange("p (u n) -> p n u", u=2),
+        )
+        wcodes = const.tile([P, 3 * P], U32, align_bytes=64)
+        wscales = const.tile([P, 3 * P], U8, align_bytes=64)
+
+        banks = {}
+        grouped = {}
+        codes = {}
+        gates = {}
+        acts = {}
+        res = {}
+        pout = {}
+
+        def transposes_half(j, half, pool, tag):
+            xw, off = half_src[2 * j + half]
+            xt = pool.tile([P, 512], F32, tag=tag)
+            for c in range(2):
+                for u in range(2):
+                    w0 = off + c * 256
+                    nc.tensor.transpose(
+                        xt[:, (2 * c + u) * P : (2 * c + u + 1) * P], xw[:, w0 + u : w0 + 256 : 2], perm[:]
+                    )
+            banks[(j, half)] = xt
+
+        def transposes(j, pool, tag):
+            transposes_half(j, 0, pool, tag)
+            transposes_half(j, 1, pool, tag)
+
+        def copy_half(j, half):
+            if half == 0:
+                gr = gpool.tile([P, 2048], BF16, tag="grouped", align_bytes=64, bufs=3)
+                grouped[j] = gr
+            gw = grouped[j][:].bitcast(F32)
+            dst = gw[:, half * 512 : (half + 1) * 512].rearrange("p (c n u) -> p c n u", c=2, u=2)
+            src = banks[(j, half)][:].rearrange("p (c u n) -> p c n u", c=2, u=2)
+            if (j, half) in SCALAR_INPUT_COPIES:
+                nc.scalar.copy(out=dst, in_=src)
+            else:
+                nc.vector.tensor_copy(out=dst, in_=src)
+
+        def quantise(j):
+            cd = gpool.tile([P, 512], U32, tag="codes", align_bytes=64)
+            sc = gpool.tile([P, 512], U8, tag="scales", align_bytes=64)
+            nc.vector.quantize_mx(out=cd[:].bitcast(FP8X4), scales=sc[:], in_=grouped[j][:])
+            codes[j] = (cd, sc)
+
+        def passes(j):
+            cd, sc = codes[j]
+            trio = {}
+            for g in (0, 2, 1):
+                pg = psg.tile([P, 512], F32, tag="gate")
+                nc.tensor.matmul_mx(
+                    out=pg[:],
+                    lhsT=wcodes[:, g * P : (g + 1) * P].bitcast(FP8X4),
+                    lhsT_scale=wscales[:, g * P : (g + 1) * P],
+                    rhs=cd[:].bitcast(FP8X4),
+                    rhs_scale=sc[:],
+                    start=True,
+                    stop=True,
+                )
+                trio[g] = pg
+            gates[j] = trio
+
+        def split(ap):
+            return ap.rearrange("p (l h) -> p l h", l=2)
+
+        def placed(tile_ap):
+            return tile_ap.rearrange("p (q l c h) -> p q l c h", q=2, l=2, c=4)
+
+        def reset_and_candidate(j, QS=(0, 1)):
+            pr = gates[j][0]
+            pn = gates[j][2]
+            r = work.tile([P, 512], F32, tag="r")
+            v = work.tile([P, 512], F32, tag="v")
+            v5 = placed(v[:])
+            for q in QS:
+                for c in range(4):
+                    b = q * 64 + 4 * j + c
+                    c0 = c * P + q * 64
+                    nc.scalar.activation(
+                        out=r[:, c0 : c0 + 64], in_=pr[:, c0 : c0 + 64], func=ACT.Sigmoid,
+                        bias=g_r[:, b : b + 1], scale=1.0,
+                    )
+                    nc.vector.scalar_tensor_tensor(
+                        out=v5[:, q, :, c, :], in0=split(r[:, c0 : c0 + 64]), scalar=h_n[:, b : b + 1],
+                        in1=split(pn[:, c0 : c0 + 64]), op0=ALU.mult, op1=ALU.add,
+                    )
+            acts[j] = [v]
+
+        def update(j, QS=(0, 1)):
+            pz = gates[j][1]
+            if QS[0] == 0:
+                zc = work.tile([P, 512], F32, tag="zc")
+                acts[j].append(zc)
+            z5 = placed(acts[j][1][:])
+            for q in QS:
+                for c in range(4):
+                    b = q * 64 + 4 * j + c
+                    c0 = c * P + q * 64
+                    nc.scalar.activation(
+                        out=z5[:, q, :, c, :], in_=split(pz[:, c0 : c0 + 64]), func=ACT.Sigmoid,
+                        bias=g_zn[:, b : b + 1], scale=-1.0,
+                    )
+
+        def candidate(j, lo=0, hi=512):
+            if lo == 0:
+                n = work.tile([P, 512], F32, tag="n", bufs=2)
+                acts[j].append(n)
+            nc.scalar.activation(
+                out=acts[j][2][:, lo:hi], in_=acts[j][0][:, lo:hi], func=ACT.Tanh, bias=bcol[:, 2:3], scale=1.0
+            )
+
+        def product(j, lo=0, hi=512):
+            v, zc, n = acts[j]
+            if lo == 0:
+                rs = work.tile([P, 512], F32, tag="rs")
+                res[j] = rs
+            if j < NU - 2:
+                nc.gpsimd.tensor_tensor(out=res[j][:, lo:hi], in0=zc[:, lo:hi], in1=n[:, lo:hi], op=ALU.mult)
+            else:
+                nc.vector.tensor_tensor(out=res[j][:, lo:hi], in0=zc[:, lo:hi], in1=n[:, lo:hi], op=ALU.mult)
+
+        def back_transposes(j):
+            po = pso.tile([P, 512], F32, tag="po")
+            for q in range(4):
+                nc.tensor.transpose(po[:, q * P : (q + 1) * P], res[j][:, q * P : (q + 1) * P], ident[:])
+            pout[j] = po
+
+        def store(j):
+            osb = work.tile([P, 512], F32, tag="osb")
+            if j in SCALAR_RESULT_COPIES:
+                nc.scalar.copy(out=osb[:], in_=pout[j][:])
+            else:
+                nc.vector.tensor_copy(out=osb[:], in_=pout[j][:])
+            nc.sync.dma_start(out=out_view[j], in_=osb[:].rearrange("p (q f) -> p q f", q=2))
+
+        def back_transposes_half(j, q):
+            ph = psx.tile([P, 512], F32, tag="xt")
+            for l in range(2):
+                nc.tensor.transpose(
+                    ph[:, l * P : (l + 1) * P], res[j][:, (2 * q + l) * P : (2 * q + l + 1) * P], ident[:]
+                )
+            pout[(j, q)] = ph
+
+        def store_half(j, q):
+            osh = work.tile([P, 256], F32, tag="osh", bufs=2)
+            if q == 0:
+                nc.vector.tensor_copy(out=osh[:], in_=pout[(j, q)][:, 0:256])
+            else:
+                nc.scalar.copy(out=osh[:], in_=pout[(j, q)][:, 0:256])
+            nc.sync.dma_start(out=out_view[j][:, q, :], in_=osh[:])
+
+        transposes(0, psx, "xt")
+        idle_matmuls(2)
+        copy_half(0, 0)
+        copy_half(0, 1)
+        for g in range(3):
+            nc.vector.quantize_mx(
+                out=wcodes[:, g * P : (g + 1) * P].bitcast(FP8X4),
+                scales=wscales[:, g * P : (g + 1) * P],
+                in_=wgrouped[:, g * I : (g + 1) * I],
+            )
+        quantise(0)
+        transposes_half(1, 0, psg, "gate")
+        pgh = psg.tile([P, 512], F32, tag="gate")
+        for g in range(4):
+            nc.tensor.transpose(pgh[:, g * P : (g + 1) * P], ghf[:, g * P : (g + 1) * P], ident[:])
+        transposes_half(1, 1, psg, "gate")
+        idle_matmuls(2)
+        bcol = const.tile([P, 4], F32)
+        nc.scalar.copy(out=bcol[:], in_=pgh[:, 384:388])
+        nbz = const.tile([P, 1], F32)
+        nc.scalar.mul(out=nbz[:], in_=pgh[:, 385:386], mul=-1.0)
+        g_r = const.tile([P, P], F32)
+        nc.scalar.activation(out=g_r[:], in_=pgh[:, 0:128], func=ACT.Identity, bias=bcol[:, 0:1], scale=1.0)
+        g_zn = const.tile([P, P], F32)
+        nc.scalar.activation(out=g_zn[:], in_=pgh[:, 128:256], func=ACT.Identity, bias=nbz[:, 0:1], scale=-1.0)
+        h_n = const.tile([P, P], F32)
+        nc.scalar.copy(out=h_n[:], in_=pgh[:, 256:384])
+        copy_half(1, 0)
+        copy_half(1, 1)
+        quantise(1)
+        passes(0)
+        transposes(2, psx, "xt")
+        passes(1)
+
+        LAST = NU - 1
+        for i in range(NU):
+            if i == 0:
+                reset_and_candidate(0)
+                copy_half(2, 0)
+                copy_half(2, 1)
+            if i + AHEAD < NU:
+                transposes(i + AHEAD, psx, "xt")
+            if i >= 1:
+                back_transposes(i - 1)
+            if 1 <= i < LAST:
+                passes(i + 1)
+            if i >= 1:
+                reset_and_candidate(i)
+            if i + AHEAD - 1 < NU:
+                quantise(i + AHEAD - 1)
+            if i + AHEAD < NU:
+                copy_half(i + AHEAD, 0)
+                copy_half(i + AHEAD, 1)
+            if i < LAST:
+                update(i)
+                candidate(i)
+            else:
+                update(i, (0,))
+                candidate(i, 0, 256)
+            if i >= 1:
+                store(i - 1)
+            if i < LAST:
+                product(i)
+        product(LAST, 0, 256)
+        update(LAST, (1,))
+        candidate(LAST, 256, 512)
+        product(LAST, 256, 512)
+        back_transposes_half(LAST, 0)
+        back_transposes_half(LAST, 1)
+        store_half(LAST, 0)
+        store_half(LAST, 1)

@@ -17,9 +17,8 @@ FLOPS = 2 * T * B * I * 3 * H
 
 NU = 16
 CHUNKS = [2, 2, 4, 8, 8, 8, 8, 8, 8, 8]
-AHEAD = 3
-SCALAR_INPUT_COPIES = ((0, 1), (2, 0))
-SCALAR_RESULT_COPIES = (0, 2, 4, 6, 8, 10)
+SCALAR_INPUT_COPIES = ((0, 1), (1, 1))
+SCALAR_RESULT_COPIES = tuple(range(NU))
 
 
 def tile_grucellmodel_pa_t_kernel(tc, input_seq, W_ih, b_ih, gh, out):
@@ -42,25 +41,27 @@ def tile_grucellmodel_pa_t_kernel(tc, input_seq, W_ih, b_ih, gh, out):
             for k in range(count):
                 nc.tensor.matmul(out=pwarm[:], lhsT=zeros[:, 0:P], rhs=zeros[:], start=True, stop=True)
 
-        idle_matmuls(8)
+        idle_matmuls(7)
 
-        ghb = const.tile([P, 512], BF16)
-        nc.vector.memset(ghb[:, 384:512], 0.0)
-        nc.scalar.dma_start(out=ghb[:, 0:384], in_=gh)
-        nc.scalar.dma_start(out=ghb[0:3, 384:512], in_=b_ih.rearrange("(g h) -> g h", g=3))
-        warm = const.tile([P, 1], F32)
-        nc.vector.memset(warm[:], 0.0)
-        warm2 = const.tile([P, 1], F32)
-        nc.scalar.activation(out=warm2[:], in_=warm[:], func=ACT.Sigmoid)
         w_sb = const.tile([P, 3 * I], BF16)
         nc.sync.dma_start(
             out=w_sb[:].rearrange("p (g k) -> p g k", g=3),
             in_=W_ih.rearrange("(g p) k -> p g k", g=3),
         )
+        warm = const.tile([P, 1], F32)
+        nc.vector.memset(warm[:], 0.0)
+        warm2 = const.tile([P, 1], F32)
+        nc.scalar.activation(out=warm2[:], in_=warm[:], func=ACT.Sigmoid)
+        brow = const.tile([P, P], BF16)
+        nc.vector.memset(brow[:], 0.0)
+        ghb = const.tile([P, 3 * H], BF16)
         xflat = input_seq.rearrange("t b k -> (t b k)").rearrange("(p f) -> p f", p=P)
         half_src = []
         bb0 = 0
         for c, nbb in enumerate(CHUNKS):
+            if c == 2:
+                nc.sync.dma_start(out=ghb[:], in_=gh)
+                nc.sync.dma_start(out=brow[0:3, :], in_=b_ih.rearrange("(g h) -> g h", g=3))
             xc = xpool.tile([P, nbb * I], BF16, name="x%d" % c)
             nc.sync.dma_start(out=xc[:], in_=xflat[:, bb0 * I : (bb0 + nbb) * I])
             for s in range(nbb // 2):
@@ -78,8 +79,8 @@ def tile_grucellmodel_pa_t_kernel(tc, input_seq, W_ih, b_ih, gh, out):
             in_=ident[:].rearrange("p (h l q) -> p q l h", q=2, l=2),
         )
 
-        ghf = const.tile([P, 512], F32)
-        nc.scalar.copy(out=ghf[:], in_=ghb[:])
+        identb = const.tile([P, P], BF16)
+        nc.vector.tensor_copy(out=identb[:], in_=ident[:])
 
         ww = w_sb[:].bitcast(F32)
         pwa = psg.tile([P, 512], F32, tag="gate")
@@ -225,7 +226,7 @@ def tile_grucellmodel_pa_t_kernel(tc, input_seq, W_ih, b_ih, gh, out):
             pout[j] = po
 
         def store(j):
-            osb = work.tile([P, 512], F32, tag="osb")
+            osb = work.tile([P, 512], F32, tag="osb", bufs=5)
             if j in SCALAR_RESULT_COPIES:
                 nc.scalar.copy(out=osb[:], in_=pout[j][:])
             else:
@@ -249,7 +250,6 @@ def tile_grucellmodel_pa_t_kernel(tc, input_seq, W_ih, b_ih, gh, out):
             nc.sync.dma_start(out=out_view[j][:, q, :], in_=osh[:])
 
         transposes(0, psx, "xt")
-        idle_matmuls(2)
         copy_half(0, 0)
         copy_half(0, 1)
         for g in range(3):
@@ -259,12 +259,10 @@ def tile_grucellmodel_pa_t_kernel(tc, input_seq, W_ih, b_ih, gh, out):
                 in_=wgrouped[:, g * I : (g + 1) * I],
             )
         quantise(0)
-        transposes_half(1, 0, psg, "gate")
-        pgh = psg.tile([P, 512], F32, tag="gate")
-        for g in range(4):
-            nc.tensor.transpose(pgh[:, g * P : (g + 1) * P], ghf[:, g * P : (g + 1) * P], ident[:])
-        transposes_half(1, 1, psg, "gate")
-        idle_matmuls(2)
+        pgh = psg.tile([P, 512], BF16, tag="gate")
+        for g in range(3):
+            nc.tensor.transpose(pgh[:, g * P : (g + 1) * P], ghb[:, g * P : (g + 1) * P], identb[:])
+        nc.tensor.transpose(pgh[:, 384:512], brow[:], identb[:])
         bcol = const.tile([P, 4], F32)
         nc.scalar.copy(out=bcol[:], in_=pgh[:, 384:388])
         nbz = const.tile([P, 1], F32)
@@ -275,32 +273,24 @@ def tile_grucellmodel_pa_t_kernel(tc, input_seq, W_ih, b_ih, gh, out):
         nc.scalar.activation(out=g_zn[:], in_=pgh[:, 128:256], func=ACT.Identity, bias=nbz[:, 0:1], scale=-1.0)
         h_n = const.tile([P, P], F32)
         nc.scalar.copy(out=h_n[:], in_=pgh[:, 256:384])
+        transposes(1, psg, "gate")
         copy_half(1, 0)
         copy_half(1, 1)
-        quantise(1)
         passes(0)
-        transposes(2, psx, "xt")
-        passes(1)
 
         LAST = NU - 1
         for i in range(NU):
-            if i == 0:
-                reset_and_candidate(0)
-                copy_half(2, 0)
-                copy_half(2, 1)
-            if i + AHEAD < NU:
-                transposes(i + AHEAD, psx, "xt")
+            if i + 2 < NU:
+                transposes(i + 2, psx, "xt")
             if i >= 1:
                 back_transposes(i - 1)
-            if 1 <= i < LAST:
+            reset_and_candidate(i)
+            if i < LAST:
+                quantise(i + 1)
                 passes(i + 1)
-            if i >= 1:
-                reset_and_candidate(i)
-            if i + AHEAD - 1 < NU:
-                quantise(i + AHEAD - 1)
-            if i + AHEAD < NU:
-                copy_half(i + AHEAD, 0)
-                copy_half(i + AHEAD, 1)
+            if i + 2 < NU:
+                copy_half(i + 2, 0)
+                copy_half(i + 2, 1)
             if i < LAST:
                 update(i)
                 candidate(i)

@@ -15,10 +15,12 @@ T, B, I, H = 64, 128, 512, 128
 P = 128
 FLOPS = 2 * T * B * I * 3 * H
 
+ROWS = tuple((q, c) for q in range(2) for c in range(4))
 NU = 16
 CHUNKS = [2, 2, 4, 8, 8, 8, 8, 8, 8, 8]
-SCALAR_INPUT_COPIES = ((0, 1), (1, 1))
-SCALAR_RESULT_COPIES = tuple(range(NU))
+FIRST = 2
+SCALAR_INPUT_COPIES = ((0, 1),) + tuple((j, 1) for j in range(FIRST, NU))
+SCALAR_RESULT_COPIES = ()
 
 
 def tile_grucellmodel_pa_t_kernel(tc, input_seq, W_ih, b_ih, gh, out):
@@ -41,13 +43,9 @@ def tile_grucellmodel_pa_t_kernel(tc, input_seq, W_ih, b_ih, gh, out):
             for k in range(count):
                 nc.tensor.matmul(out=pwarm[:], lhsT=zeros[:, 0:P], rhs=zeros[:], start=True, stop=True)
 
-        idle_matmuls(7)
+        idle_matmuls(5)
 
         w_sb = const.tile([P, 3 * I], BF16)
-        nc.sync.dma_start(
-            out=w_sb[:].rearrange("p (g k) -> p g k", g=3),
-            in_=W_ih.rearrange("(g p) k -> p g k", g=3),
-        )
         warm = const.tile([P, 1], F32)
         nc.vector.memset(warm[:], 0.0)
         warm2 = const.tile([P, 1], F32)
@@ -59,14 +57,20 @@ def tile_grucellmodel_pa_t_kernel(tc, input_seq, W_ih, b_ih, gh, out):
         half_src = []
         bb0 = 0
         for c, nbb in enumerate(CHUNKS):
-            if c == 2:
-                nc.sync.dma_start(out=ghb[:], in_=gh)
-                nc.sync.dma_start(out=brow[0:3, :], in_=b_ih.rearrange("(g h) -> g h", g=3))
             xc = xpool.tile([P, nbb * I], BF16, name="x%d" % c)
             nc.sync.dma_start(out=xc[:], in_=xflat[:, bb0 * I : (bb0 + nbb) * I])
             for s in range(nbb // 2):
                 half_src.append((xc[:].bitcast(F32), s * 2 * 256))
             bb0 += nbb
+            if c == 0:
+                nc.sync.dma_start(out=w_sb[:, 0:I], in_=W_ih[0:P, :])
+            if c == 1:
+                nc.sync.dma_start(
+                    out=w_sb[:, I : 3 * I].rearrange("p (g k) -> p g k", g=2),
+                    in_=W_ih[P : 3 * P, :].rearrange("(g p) k -> p g k", g=2),
+                )
+                nc.sync.dma_start(out=ghb[:], in_=gh)
+                nc.sync.dma_start(out=brow[0:3, :], in_=b_ih.rearrange("(g h) -> g h", g=3))
         out_view = out.rearrange("b t h -> (b t h)").rearrange(
             "(q j i f) -> j i q f", q=2, j=NU, i=P
         )
@@ -83,22 +87,34 @@ def tile_grucellmodel_pa_t_kernel(tc, input_seq, W_ih, b_ih, gh, out):
         nc.vector.tensor_copy(out=identb[:], in_=ident[:])
 
         ww = w_sb[:].bitcast(F32)
-        pwa = psg.tile([P, 512], F32, tag="gate")
-        pwb = psg.tile([P, 512], F32, tag="gate")
-        for g in range(3):
-            for u in range(2):
-                dst = pwa[:, (2 * g + u) * P : (2 * g + u + 1) * P] if g < 2 else pwb[:, u * P : (u + 1) * P]
-                nc.tensor.transpose(dst, ww[:, g * 256 + u : (g + 1) * 256 : 2], ident[:])
         wgrouped = const.tile([P, 3 * I], BF16, align_bytes=64)
         wgw = wgrouped[:].bitcast(F32)
-        nc.vector.tensor_copy(
-            out=wgw[:, 0:512].rearrange("p (c n u) -> p c n u", c=2, u=2),
-            in_=pwa[:].rearrange("p (c u n) -> p c n u", c=2, u=2),
-        )
-        nc.scalar.copy(
-            out=wgw[:, 512:768].rearrange("p (n u) -> p n u", u=2),
-            in_=pwb[:, 0:256].rearrange("p (u n) -> p n u", u=2),
-        )
+        wbank = {}
+
+        def weight_transposes(gs):
+            pw = psg.tile([P, 512], F32, tag="gate")
+            for c, g in enumerate(gs):
+                for u in range(2):
+                    nc.tensor.transpose(
+                        pw[:, (2 * c + u) * P : (2 * c + u + 1) * P], ww[:, g * 256 + u : (g + 1) * 256 : 2], ident[:]
+                    )
+            wbank[gs] = pw
+
+        def weight_copy(gs):
+            n = len(gs)
+            nc.scalar.copy(
+                out=wgw[:, gs[0] * 256 : (gs[0] + n) * 256].rearrange("p (c n u) -> p c n u", c=n, u=2),
+                in_=wbank[gs][:, 0 : n * 256].rearrange("p (c u n) -> p c n u", c=n, u=2),
+            )
+
+        def weight_quantise(gs):
+            for g in gs:
+                nc.vector.quantize_mx(
+                    out=wcodes[:, g * P : (g + 1) * P].bitcast(FP8X4),
+                    scales=wscales[:, g * P : (g + 1) * P],
+                    in_=wgrouped[:, g * I : (g + 1) * I],
+                )
+
         wcodes = const.tile([P, 3 * P], U32, align_bytes=64)
         wscales = const.tile([P, 3 * P], U8, align_bytes=64)
 
@@ -126,7 +142,7 @@ def tile_grucellmodel_pa_t_kernel(tc, input_seq, W_ih, b_ih, gh, out):
             transposes_half(j, 1, pool, tag)
 
         def copy_half(j, half):
-            if half == 0:
+            if j not in grouped:
                 gr = gpool.tile([P, 2048], BF16, tag="grouped", align_bytes=64, bufs=3)
                 grouped[j] = gr
             gw = grouped[j][:].bitcast(F32)
@@ -166,32 +182,38 @@ def tile_grucellmodel_pa_t_kernel(tc, input_seq, W_ih, b_ih, gh, out):
         def placed(tile_ap):
             return tile_ap.rearrange("p (q l c h) -> p q l c h", q=2, l=2, c=4)
 
-        def reset_and_candidate(j, QS=(0, 1)):
+        def reset(j):
             pr = gates[j][0]
-            pn = gates[j][2]
             r = work.tile([P, 512], F32, tag="r")
+            for q, c in ROWS:
+                b = q * 64 + 4 * j + c
+                c0 = c * P + q * 64
+                nc.scalar.activation(
+                    out=r[:, c0 : c0 + 64], in_=pr[:, c0 : c0 + 64], func=ACT.Sigmoid,
+                    bias=g_r[:, b : b + 1], scale=1.0,
+                )
+            acts[j] = {"r": r}
+
+        def preactivation(j):
+            pn = gates[j][2]
+            r = acts[j]["r"]
             v = work.tile([P, 512], F32, tag="v")
             v5 = placed(v[:])
-            for q in QS:
-                for c in range(4):
-                    b = q * 64 + 4 * j + c
-                    c0 = c * P + q * 64
-                    nc.scalar.activation(
-                        out=r[:, c0 : c0 + 64], in_=pr[:, c0 : c0 + 64], func=ACT.Sigmoid,
-                        bias=g_r[:, b : b + 1], scale=1.0,
-                    )
-                    nc.vector.scalar_tensor_tensor(
-                        out=v5[:, q, :, c, :], in0=split(r[:, c0 : c0 + 64]), scalar=h_n[:, b : b + 1],
-                        in1=split(pn[:, c0 : c0 + 64]), op0=ALU.mult, op1=ALU.add,
-                    )
-            acts[j] = [v]
+            for q, c in ROWS:
+                b = q * 64 + 4 * j + c
+                c0 = c * P + q * 64
+                nc.vector.scalar_tensor_tensor(
+                    out=v5[:, q, :, c, :], in0=split(r[:, c0 : c0 + 64]), scalar=h_n[:, b : b + 1],
+                    in1=split(pn[:, c0 : c0 + 64]), op0=ALU.mult, op1=ALU.add,
+                )
+            acts[j]["v"] = v
 
         def update(j, QS=(0, 1)):
             pz = gates[j][1]
             if QS[0] == 0:
                 zc = work.tile([P, 512], F32, tag="zc")
-                acts[j].append(zc)
-            z5 = placed(acts[j][1][:])
+                acts[j]["zc"] = zc
+            z5 = placed(acts[j]["zc"][:])
             for q in QS:
                 for c in range(4):
                     b = q * 64 + 4 * j + c
@@ -204,13 +226,13 @@ def tile_grucellmodel_pa_t_kernel(tc, input_seq, W_ih, b_ih, gh, out):
         def candidate(j, lo=0, hi=512):
             if lo == 0:
                 n = work.tile([P, 512], F32, tag="n", bufs=2)
-                acts[j].append(n)
+                acts[j]["n"] = n
             nc.scalar.activation(
-                out=acts[j][2][:, lo:hi], in_=acts[j][0][:, lo:hi], func=ACT.Tanh, bias=bcol[:, 2:3], scale=1.0
+                out=acts[j]["n"][:, lo:hi], in_=acts[j]["v"][:, lo:hi], func=ACT.Tanh, bias=bcol[:, 2:3], scale=1.0
             )
 
         def product(j, lo=0, hi=512):
-            v, zc, n = acts[j]
+            zc, n = acts[j]["zc"], acts[j]["n"]
             if lo == 0:
                 rs = work.tile([P, 512], F32, tag="rs")
                 res[j] = rs
@@ -249,16 +271,17 @@ def tile_grucellmodel_pa_t_kernel(tc, input_seq, W_ih, b_ih, gh, out):
                 nc.scalar.copy(out=osh[:], in_=pout[(j, q)][:, 0:256])
             nc.sync.dma_start(out=out_view[j][:, q, :], in_=osh[:])
 
-        transposes(0, psx, "xt")
+        transposes_half(0, 0, psx, "xt")
+        weight_transposes((0,))
+        transposes_half(0, 1, psx, "xt")
         copy_half(0, 0)
+        weight_copy((0,))
         copy_half(0, 1)
-        for g in range(3):
-            nc.vector.quantize_mx(
-                out=wcodes[:, g * P : (g + 1) * P].bitcast(FP8X4),
-                scales=wscales[:, g * P : (g + 1) * P],
-                in_=wgrouped[:, g * I : (g + 1) * I],
-            )
+        weight_quantise((0,))
+        weight_transposes((1, 2))
+        weight_copy((1, 2))
         quantise(0)
+        weight_quantise((2, 1))
         pgh = psg.tile([P, 512], BF16, tag="gate")
         for g in range(3):
             nc.tensor.transpose(pgh[:, g * P : (g + 1) * P], ghb[:, g * P : (g + 1) * P], identb[:])
@@ -284,21 +307,22 @@ def tile_grucellmodel_pa_t_kernel(tc, input_seq, W_ih, b_ih, gh, out):
                 transposes(i + 2, psx, "xt")
             if i >= 1:
                 back_transposes(i - 1)
-            reset_and_candidate(i)
+            reset(i)
+            preactivation(i)
             if i < LAST:
                 quantise(i + 1)
+            if i < LAST:
                 passes(i + 1)
             if i + 2 < NU:
                 copy_half(i + 2, 0)
+            if i + 2 < min(FIRST, NU):
                 copy_half(i + 2, 1)
-            if i < LAST:
-                update(i)
-                candidate(i)
-            else:
-                update(i, (0,))
-                candidate(i, 0, 256)
             if i >= 1:
                 store(i - 1)
+            update(i) if i < LAST else update(i, (0,))
+            candidate(i) if i < LAST else candidate(i, 0, 256)
+            if FIRST <= i + 2 < NU:
+                copy_half(i + 2, 1)
             if i < LAST:
                 product(i)
         product(LAST, 0, 256)

@@ -156,7 +156,12 @@ def tile_grucellmodel_pa_t_kernel(tc, input_seq, W_ih, b_ih, gh, out):
         def quantise(j):
             cd = gpool.tile([P, 512], U32, tag="codes", align_bytes=64)
             sc = gpool.tile([P, 512], U8, tag="scales", align_bytes=64)
-            nc.vector.quantize_mx(out=cd[:].bitcast(FP8X4), scales=sc[:], in_=grouped[j][:])
+            for s in range(2):
+                nc.vector.quantize_mx(
+                    out=cd[:, s * 256 : (s + 1) * 256].bitcast(FP8X4),
+                    scales=sc[:, s * 256 : (s + 1) * 256],
+                    in_=grouped[j][:, s * 1024 : (s + 1) * 1024],
+                )
             codes[j] = (cd, sc)
 
         def passes(j):
@@ -164,15 +169,17 @@ def tile_grucellmodel_pa_t_kernel(tc, input_seq, W_ih, b_ih, gh, out):
             trio = {}
             for g in (0, 2, 1):
                 pg = psg.tile([P, 512], F32, tag="gate")
-                nc.tensor.matmul_mx(
-                    out=pg[:],
-                    lhsT=wcodes[:, g * P : (g + 1) * P].bitcast(FP8X4),
-                    lhsT_scale=wscales[:, g * P : (g + 1) * P],
-                    rhs=cd[:].bitcast(FP8X4),
-                    rhs_scale=sc[:],
-                    start=True,
-                    stop=True,
-                )
+                for s in range(2) if g == 0 else (None,):
+                    cols = slice(0, 512) if s is None else slice(s * 256, (s + 1) * 256)
+                    nc.tensor.matmul_mx(
+                        out=pg[:, cols],
+                        lhsT=wcodes[:, g * P : (g + 1) * P].bitcast(FP8X4),
+                        lhsT_scale=wscales[:, g * P : (g + 1) * P],
+                        rhs=cd[:, cols].bitcast(FP8X4),
+                        rhs_scale=sc[:, cols],
+                        start=True,
+                        stop=True,
+                    )
                 trio[g] = pg
             gates[j] = trio
 

@@ -15,10 +15,10 @@ T, B, I, H = 64, 128, 512, 128
 P = 128
 FLOPS = 2 * T * B * I * 3 * H
 
-ROWS = tuple((q, c) for q in range(2) for c in range(4))
+ROWS = tuple((q, c) for c in range(4) for q in range(2))
 NU = 16
 CHUNKS = [2, 2, 4, 8, 8, 8, 8, 8, 8, 8]
-FIRST = 2
+FIRST = 3
 SCALAR_INPUT_COPIES = ((0, 1),) + tuple((j, 1) for j in range(FIRST, NU))
 SCALAR_RESULT_COPIES = ()
 
@@ -166,22 +166,21 @@ def tile_grucellmodel_pa_t_kernel(tc, input_seq, W_ih, b_ih, gh, out):
 
         def passes(j):
             cd, sc = codes[j]
-            trio = {}
-            for g in (0, 2, 1):
+            parts = {}
+            for g, s in ((0, 0), (2, 0), (0, 1), (2, 1), (1, None)):
+                cols = slice(0, 512) if s is None else slice(s * 256, (s + 1) * 256)
                 pg = psg.tile([P, 512], F32, tag="gate")
-                for s in range(2) if g == 0 else (None,):
-                    cols = slice(0, 512) if s is None else slice(s * 256, (s + 1) * 256)
-                    nc.tensor.matmul_mx(
-                        out=pg[:, cols],
-                        lhsT=wcodes[:, g * P : (g + 1) * P].bitcast(FP8X4),
-                        lhsT_scale=wscales[:, g * P : (g + 1) * P],
-                        rhs=cd[:, cols].bitcast(FP8X4),
-                        rhs_scale=sc[:, cols],
-                        start=True,
-                        stop=True,
-                    )
-                trio[g] = pg
-            gates[j] = trio
+                nc.tensor.matmul_mx(
+                    out=pg[:, 0 : cols.stop - cols.start],
+                    lhsT=wcodes[:, g * P : (g + 1) * P].bitcast(FP8X4),
+                    lhsT_scale=wscales[:, g * P : (g + 1) * P],
+                    rhs=cd[:, cols].bitcast(FP8X4),
+                    rhs_scale=sc[:, cols],
+                    start=True,
+                    stop=True,
+                )
+                parts[(g, s)] = pg
+            gates[j] = parts
 
         def split(ap):
             return ap.rearrange("p (l h) -> p l h", l=2)
@@ -190,19 +189,17 @@ def tile_grucellmodel_pa_t_kernel(tc, input_seq, W_ih, b_ih, gh, out):
             return tile_ap.rearrange("p (q l c h) -> p q l c h", q=2, l=2, c=4)
 
         def reset(j):
-            pr = gates[j][0]
             r = work.tile([P, 512], F32, tag="r")
             for q, c in ROWS:
                 b = q * 64 + 4 * j + c
                 c0 = c * P + q * 64
                 nc.scalar.activation(
-                    out=r[:, c0 : c0 + 64], in_=pr[:, c0 : c0 + 64], func=ACT.Sigmoid,
+                    out=r[:, c0 : c0 + 64], in_=gates[j][(0, c // 2)][:, c0 % 256 : c0 % 256 + 64], func=ACT.Sigmoid,
                     bias=g_r[:, b : b + 1], scale=1.0,
                 )
             acts[j] = {"r": r}
 
         def preactivation(j):
-            pn = gates[j][2]
             r = acts[j]["r"]
             v = work.tile([P, 512], F32, tag="v")
             v5 = placed(v[:])
@@ -211,12 +208,12 @@ def tile_grucellmodel_pa_t_kernel(tc, input_seq, W_ih, b_ih, gh, out):
                 c0 = c * P + q * 64
                 nc.vector.scalar_tensor_tensor(
                     out=v5[:, q, :, c, :], in0=split(r[:, c0 : c0 + 64]), scalar=h_n[:, b : b + 1],
-                    in1=split(pn[:, c0 : c0 + 64]), op0=ALU.mult, op1=ALU.add,
+                    in1=split(gates[j][(2, c // 2)][:, c0 % 256 : c0 % 256 + 64]), op0=ALU.mult, op1=ALU.add,
                 )
             acts[j]["v"] = v
 
         def update(j, QS=(0, 1)):
-            pz = gates[j][1]
+            pz = gates[j][(1, None)]
             if QS[0] == 0:
                 zc = work.tile([P, 512], F32, tag="zc")
                 acts[j]["zc"] = zc

@@ -17,7 +17,7 @@ FLOPS = 2 * T * B * I * 3 * H
 
 ROWS = tuple((q, c) for c in range(4) for q in range(2))
 NU = 16
-CHUNKS = [2, 2, 4, 8, 8, 8, 8, 8, 8, 8]
+CHUNKS = [2, 2, 2, 2, 4, 4, 8, 8, 8, 8, 8, 8]
 FIRST = 3
 SCALAR_INPUT_COPIES = ((0, 1),) + tuple((j, 1) for j in range(FIRST, NU))
 SCALAR_RESULT_COPIES = ()
@@ -300,7 +300,8 @@ def tile_grucellmodel_pa_t_kernel(tc, input_seq, W_ih, b_ih, gh, out):
         nc.scalar.activation(out=g_zn[:], in_=pgh[:, 128:256], func=ACT.Identity, bias=nbz[:, 0:1], scale=-1.0)
         h_n = const.tile([P, P], F32)
         nc.scalar.copy(out=h_n[:], in_=pgh[:, 256:384])
-        transposes(1, psg, "gate")
+        transposes_half(1, 0, psx, "xt")
+        transposes_half(1, 1, psx, "xt")
         copy_half(1, 0)
         copy_half(1, 1)
         passes(0)

from contextlib import ExitStack

import concourse.mybir as mybir
from concourse.masks import make_identity

F32 = mybir.dt.float32
BF16 = mybir.dt.bfloat16
U32 = mybir.dt.uint32
U8 = mybir.dt.uint8
FP8X4 = mybir.dt.float8_e4m3fn_x4
ACT = mybir.ActivationFunctionType
ALU = mybir.AluOpType

T, B, I, H = 64, 128, 512, 128
P = 128
FLOPS = 2 * T * B * I * 3 * H

ROWS = tuple((q, c) for c in range(4) for q in range(2))
NU = 16
CHUNKS = [2, 2, 2, 2, 4, 4, 8, 8, 8, 8, 8, 8]
FIRST = 3
SCALAR_INPUT_COPIES = ((0, 1),) + tuple((j, 1) for j in range(FIRST, NU))
SCALAR_RESULT_COPIES = ()


def tile_grucellmodel_pa_t_kernel(tc, input_seq, W_ih, b_ih, gh, out):
    nc = tc.nc
    with ExitStack() as ctx:
        const = ctx.enter_context(tc.tile_pool(name="const", bufs=1))
        xpool = ctx.enter_context(tc.tile_pool(name="xpool", bufs=1))
        gpool = ctx.enter_context(tc.tile_pool(name="gpool", bufs=4))
        work = ctx.enter_context(tc.tile_pool(name="work", bufs=3))
        psx = ctx.enter_context(tc.psum_pool(name="psx", bufs=2))
        psg = ctx.enter_context(tc.psum_pool(name="psg", bufs=5))
        pso = ctx.enter_context(tc.psum_pool(name="pso", bufs=1))
        ctx.enter_context(tc.manual_schedule())

        zeros = const.tile([P, 512], BF16)
        nc.vector.memset(zeros[:], 0.0)
        pwarm = pso.tile([P, 512], F32, tag="po")

        def idle_matmuls(count):
            for k in range(count):
                nc.tensor.matmul(out=pwarm[:], lhsT=zeros[:, 0:P], rhs=zeros[:], start=True, stop=True)

        idle_matmuls(5)

        w_sb = const.tile([P, 3 * I], BF16)
        warm = const.tile([P, 1], F32)
        nc.vector.memset(warm[:], 0.0)
        warm2 = const.tile([P, 1], F32)
        nc.scalar.activation(out=warm2[:], in_=warm[:], func=ACT.Sigmoid)
        brow = const.tile([P, P], BF16)
        nc.vector.memset(brow[:], 0.0)
        ghb = const.tile([P, 3 * H], BF16)
        xflat = input_seq.rearrange("t b k -> (t b k)").rearrange("(p f) -> p f", p=P)
        half_src = []
        bb0 = 0
        for c, nbb in enumerate(CHUNKS):
            xc = xpool.tile([P, nbb * I], BF16, name="x%d" % c)
            nc.sync.dma_start(out=xc[:], in_=xflat[:, bb0 * I : (bb0 + nbb) * I])
            for s in range(nbb // 2):
                half_src.append((xc[:].bitcast(F32), s * 2 * 256))
            bb0 += nbb
            if c == 0:
                nc.sync.dma_start(out=w_sb[:, 0:I], in_=W_ih[0:P, :])
            if c == 1:
                nc.sync.dma_start(
                    out=w_sb[:, I : 3 * I].rearrange("p (g k) -> p g k", g=2),
                    in_=W_ih[P : 3 * P, :].rearrange("(g p) k -> p g k", g=2),
                )
                nc.sync.dma_start(out=ghb[:], in_=gh)
                nc.sync.dma_start(out=brow[0:3, :], in_=b_ih.rearrange("(g h) -> g h", g=3))
        out_view = out.rearrange("b t h -> (b t h)").rearrange(
            "(q j i f) -> j i q f", q=2, j=NU, i=P
        )

        ident = const.tile([P, P], F32)
        make_identity(nc, ident[:])
        perm = const.tile([P, P], F32)
        nc.vector.tensor_copy(
            out=perm[:].rearrange("p (q l h) -> p q l h", q=2, l=2),
            in_=ident[:].rearrange("p (h l q) -> p q l h", q=2, l=2),
        )

        identb = const.tile([P, P], BF16)
        nc.vector.tensor_copy(out=identb[:], in_=ident[:])

        ww = w_sb[:].bitcast(F32)
        wgrouped = const.tile([P, 3 * I], BF16, align_bytes=64)
        wgw = wgrouped[:].bitcast(F32)
        wbank = {}

        def weight_transposes(gs):
            pw = psg.tile([P, 512], F32, tag="gate")
            for c, g in enumerate(gs):
                for u in range(2):
                    nc.tensor.transpose(
                        pw[:, (2 * c + u) * P : (2 * c + u + 1) * P], ww[:, g * 256 + u : (g + 1) * 256 : 2], ident[:]
                    )
            wbank[gs] = pw

        def weight_copy(gs):
            n = len(gs)
            nc.scalar.copy(
                out=wgw[:, gs[0] * 256 : (gs[0] + n) * 256].rearrange("p (c n u) -> p c n u", c=n, u=2),
                in_=wbank[gs][:, 0 : n * 256].rearrange("p (c u n) -> p c n u", c=n, u=2),
            )

        def weight_quantise(gs):
            for g in gs:
                nc.vector.quantize_mx(
                    out=wcodes[:, g * P : (g + 1) * P].bitcast(FP8X4),
                    scales=wscales[:, g * P : (g + 1) * P],
                    in_=wgrouped[:, g * I : (g + 1) * I],
                )

        wcodes = const.tile([P, 3 * P], U32, align_bytes=64)
        wscales = const.tile([P, 3 * P], U8, align_bytes=64)

        banks = {}
        grouped = {}
        codes = {}
        gates = {}
        acts = {}
        res = {}
        pout = {}

        def transposes_half(j, half, pool, tag):
            xw, off = half_src[2 * j + half]
            xt = pool.tile([P, 512], F32, tag=tag)
            for c in range(2):
                for u in range(2):
                    w0 = off + c * 256
                    nc.tensor.transpose(
                        xt[:, (2 * c + u) * P : (2 * c + u + 1) * P], xw[:, w0 + u : w0 + 256 : 2], perm[:]
                    )
            banks[(j, half)] = xt

        def transposes(j, pool, tag):
            transposes_half(j, 0, pool, tag)
            transposes_half(j, 1, pool, tag)

        def copy_half(j, half):
            if j not in grouped:
                gr = gpool.tile([P, 2048], BF16, tag="grouped", align_bytes=64, bufs=3)
                grouped[j] = gr
            gw = grouped[j][:].bitcast(F32)
            dst = gw[:, half * 512 : (half + 1) * 512].rearrange("p (c n u) -> p c n u", c=2, u=2)
            src = banks[(j, half)][:].rearrange("p (c u n) -> p c n u", c=2, u=2)
            if (j, half) in SCALAR_INPUT_COPIES:
                nc.scalar.copy(out=dst, in_=src)
            else:
                nc.vector.tensor_copy(out=dst, in_=src)

        def quantise(j):
            cd = gpool.tile([P, 512], U32, tag="codes", align_bytes=64)
            sc = gpool.tile([P, 512], U8, tag="scales", align_bytes=64)
            for s in range(2):
                nc.vector.quantize_mx(
                    out=cd[:, s * 256 : (s + 1) * 256].bitcast(FP8X4),
                    scales=sc[:, s * 256 : (s + 1) * 256],
                    in_=grouped[j][:, s * 1024 : (s + 1) * 1024],
                )
            codes[j] = (cd, sc)

        def passes(j):
            cd, sc = codes[j]
            parts = {}
            for g, s in ((0, 0), (2, 0), (0, 1), (2, 1), (1, None)):
                cols = slice(0, 512) if s is None else slice(s * 256, (s + 1) * 256)
                pg = psg.tile([P, 512], F32, tag="gate")
                nc.tensor.matmul_mx(
                    out=pg[:, 0 : cols.stop - cols.start],
                    lhsT=wcodes[:, g * P : (g + 1) * P].bitcast(FP8X4),
                    lhsT_scale=wscales[:, g * P : (g + 1) * P],
                    rhs=cd[:, cols].bitcast(FP8X4),
                    rhs_scale=sc[:, cols],
                    start=True,
                    stop=True,
                )
                parts[(g, s)] = pg
            gates[j] = parts

        def split(ap):
            return ap.rearrange("p (l h) -> p l h", l=2)

        def placed(tile_ap):
            return tile_ap.rearrange("p (q l c h) -> p q l c h", q=2, l=2, c=4)

        def reset(j):
            r = work.tile([P, 512], F32, tag="r")
            for q, c in ROWS:
                b = q * 64 + 4 * j + c
                c0 = c * P + q * 64
                nc.scalar.activation(
                    out=r[:, c0 : c0 + 64], in_=gates[j][(0, c // 2)][:, c0 % 256 : c0 % 256 + 64], func=ACT.Sigmoid,
                    bias=g_r[:, b : b + 1], scale=1.0,
                )
            acts[j] = {"r": r}

        def preactivation(j):
            r = acts[j]["r"]
            v = work.tile([P, 512], F32, tag="v")
            v5 = placed(v[:])
            for q, c in ROWS:
                b = q * 64 + 4 * j + c
                c0 = c * P + q * 64
                nc.vector.scalar_tensor_tensor(
                    out=v5[:, q, :, c, :], in0=split(r[:, c0 : c0 + 64]), scalar=h_n[:, b : b + 1],
                    in1=split(gates[j][(2, c // 2)][:, c0 % 256 : c0 % 256 + 64]), op0=ALU.mult, op1=ALU.add,
                )
            acts[j]["v"] = v

        def update(j, QS=(0, 1)):
            pz = gates[j][(1, None)]
            if QS[0] == 0:
                zc = work.tile([P, 512], F32, tag="zc")
                acts[j]["zc"] = zc
            z5 = placed(acts[j]["zc"][:])
            for q in QS:
                for c in range(4):
                    b = q * 64 + 4 * j + c
                    c0 = c * P + q * 64
                    nc.scalar.activation(
                        out=z5[:, q, :, c, :], in_=split(pz[:, c0 : c0 + 64]), func=ACT.Sigmoid,
                        bias=g_zn[:, b : b + 1], scale=-1.0,
                    )

        def candidate(j, lo=0, hi=512):
            if lo == 0:
                n = work.tile([P, 512], F32, tag="n", bufs=2)
                acts[j]["n"] = n
            nc.scalar.activation(
                out=acts[j]["n"][:, lo:hi], in_=acts[j]["v"][:, lo:hi], func=ACT.Tanh, bias=bcol[:, 2:3], scale=1.0
            )

        def product(j, lo=0, hi=512):
            zc, n = acts[j]["zc"], acts[j]["n"]
            if lo == 0:
                rs = work.tile([P, 512], F32, tag="rs")
                res[j] = rs
            if j < NU - 2:
                nc.gpsimd.tensor_tensor(out=res[j][:, lo:hi], in0=zc[:, lo:hi], in1=n[:, lo:hi], op=ALU.mult)
            else:
                nc.vector.tensor_tensor(out=res[j][:, lo:hi], in0=zc[:, lo:hi], in1=n[:, lo:hi], op=ALU.mult)

        def back_transposes(j):
            po = pso.tile([P, 512], F32, tag="po")
            for q in range(4):
                nc.tensor.transpose(po[:, q * P : (q + 1) * P], res[j][:, q * P : (q + 1) * P], ident[:])
            pout[j] = po

        def store(j):
            osb = work.tile([P, 512], F32, tag="osb", bufs=5)
            if j in SCALAR_RESULT_COPIES:
                nc.scalar.copy(out=osb[:], in_=pout[j][:])
            else:
                nc.vector.tensor_copy(out=osb[:], in_=pout[j][:])
            nc.sync.dma_start(out=out_view[j], in_=osb[:].rearrange("p (q f) -> p q f", q=2))

        def back_transposes_half(j, q):
            ph = psx.tile([P, 512], F32, tag="xt")
            for l in range(2):
                nc.tensor.transpose(
                    ph[:, l * P : (l + 1) * P], res[j][:, (2 * q + l) * P : (2 * q + l + 1) * P], ident[:]
                )
            pout[(j, q)] = ph

        def store_half(j, q):
            osh = work.tile([P, 256], F32, tag="osh", bufs=2)
            if q == 0:
                nc.vector.tensor_copy(out=osh[:], in_=pout[(j, q)][:, 0:256])
            else:
                nc.scalar.copy(out=osh[:], in_=pout[(j, q)][:, 0:256])
            nc.sync.dma_start(out=out_view[j][:, q, :], in_=osh[:])

        transposes_half(0, 0, psx, "xt")
        weight_transposes((0,))
        transposes_half(0, 1, psx, "xt")
        copy_half(0, 0)
        weight_copy((0,))
        copy_half(0, 1)
        weight_quantise((0,))
        weight_transposes((1, 2))
        weight_copy((1, 2))
        quantise(0)
        weight_quantise((2, 1))
        pgh = psg.tile([P, 512], BF16, tag="gate")
        for g in range(3):
            nc.tensor.transpose(pgh[:, g * P : (g + 1) * P], ghb[:, g * P : (g + 1) * P], identb[:])
        nc.tensor.transpose(pgh[:, 384:512], brow[:], identb[:])
        bcol = const.tile([P, 4], F32)
        nc.scalar.copy(out=bcol[:], in_=pgh[:, 384:388])
        nbz = const.tile([P, 1], F32)
        nc.scalar.mul(out=nbz[:], in_=pgh[:, 385:386], mul=-1.0)
        g_r = const.tile([P, P], F32)
        nc.scalar.activation(out=g_r[:], in_=pgh[:, 0:128], func=ACT.Identity, bias=bcol[:, 0:1], scale=1.0)
        g_zn = const.tile([P, P], F32)
        nc.scalar.activation(out=g_zn[:], in_=pgh[:, 128:256], func=ACT.Identity, bias=nbz[:, 0:1], scale=-1.0)
        h_n = const.tile([P, P], F32)
        nc.scalar.copy(out=h_n[:], in_=pgh[:, 256:384])
        transposes_half(1, 0, psx, "xt")
        transposes_half(1, 1, psx, "xt")
        copy_half(1, 0)
        copy_half(1, 1)
        passes(0)

        LAST = NU - 1
        for i in range(NU):
            if i + 2 < NU:
                transposes(i + 2, psx, "xt")
            if i >= 1:
                back_transposes(i - 1)
            reset(i)
            preactivation(i)
            if i < LAST:
                quantise(i + 1)
            if i < LAST:
                passes(i + 1)
            if i + 2 < NU:
                copy_half(i + 2, 0)
            if i + 2 < min(FIRST, NU):
                copy_half(i + 2, 1)
            if i >= 1:
                store(i - 1)
            update(i) if i < LAST else update(i, (0,))
            candidate(i) if i < LAST else candidate(i, 0, 256)
            if FIRST <= i + 2 < NU:
                copy_half(i + 2, 1)
            if i < LAST:
                product(i)
        product(LAST, 0, 256)
        update(LAST, (1,))
        candidate(LAST, 256, 512)
        product(LAST, 256, 512)
        back_transposes_half(LAST, 0)
        back_transposes_half(LAST, 1)
        store_half(LAST, 0)
        store_half(LAST, 1)
